import numpy as np
import ml_dtypes


def mxq(x, axis, fmt="e4m3"):
    dtype, down = {"e4m3": (ml_dtypes.float8_e4m3fn, 7), "e5m2": (ml_dtypes.float8_e5m2, 14)}[fmt]
    v = np.moveaxis(np.asarray(x, np.float32).astype(ml_dtypes.bfloat16).astype(np.float64), axis, -1)
    blocks = v.reshape(v.shape[:-1] + (-1, 32))
    amax = np.abs(blocks).max(-1, keepdims=True)
    byte = np.maximum(np.where(amax > 0, np.frexp(amax)[1] - 1 + 127, 0) - down, 1)
    scale = np.exp2(byte - 127.0)
    codes = (blocks / scale).astype(np.float32).astype(dtype).astype(np.float64)
    return np.moveaxis((codes * scale).reshape(v.shape), -1, axis)


WIDE = False


def mx_kscale(k):
    if not WIDE:
        return np.ones(k)
    levels = np.array([10, -10, 5, -5, 0])
    if k % 512:
        return np.exp2(np.random.permutation(np.resize(levels, k // 32))).repeat(32)
    a = np.empty((k // 512, 16))
    for p in range(k // 512):
        a[p, :8] = np.random.permutation(np.resize(levels, 8))
        for g in range(8):
            far = levels[np.abs(levels - a[p, g]) >= 10]
            a[p, g + 8] = far[np.random.randint(len(far))]
    return np.exp2(a.ravel()).repeat(32)


BF16 = ml_dtypes.bfloat16


def bf(x):
    return np.asarray(x, np.float32).astype(BF16)


def f64(x):
    return np.asarray(x).astype(np.float64)


B, T, D, H = 8, 1024, 512, 2048
R = B * T


def sigmoid(v):
    return 1.0 / (1.0 + np.exp(-v))


def setup_inputs():
    s, t = mx_kscale(D), mx_kscale(D)
    n = np.random.standard_normal
    return {"h": bf(n((B, T, D)) * s), "yt": bf(n((B, T, D)) * 0.5 * t),
            "Wq": bf(n((D, D)) * 1.5 / np.sqrt(D) / s[:, None]), "bq": bf(0.3 * n(D)),
            "Wo": bf(n((D, D)) * 2.5 / np.sqrt(D) / t[:, None]), "bo": bf(0.3 * n(D))}


def reference(h, yt, Wq, bq, Wo, bo):
    q = (mxq(f64(h).reshape(R, D), 1, "e4m3") @ mxq(f64(Wq), 0, "e4m3")) + f64(bq)
    y = sigmoid(q) * f64(yt).reshape(R, D)
    attn = (mxq(y, 1, "e4m3") @ mxq(f64(Wo), 0, "e4m3")) + f64(bo)
    return attn.reshape(B, T, D)

@@ -1,0 +1,277 @@
+from contextlib import ExitStack
+
+import concourse.mybir as mybir
+from concourse.masks import make_identity
+
+F32 = mybir.dt.float32
+BF16 = mybir.dt.bfloat16
+U32 = mybir.dt.uint32
+U8 = mybir.dt.uint8
+FP8X4 = mybir.dt.float8_e4m3fn_x4
+SIGMOID = mybir.ActivationFunctionType.Sigmoid
+ADD = mybir.AluOpType.add
+MULT = mybir.AluOpType.mult
+
+ROWS = 8 * 1024
+D = 512
+P = 128
+PACK = 4
+CHUNK = 512
+CHUNKS = ROWS // CHUNK
+ROW_TILES = CHUNK // P
+HALF = CHUNK // 2
+BANK = 512
+LOOKAHEAD = 3
+
+AT_QUANTISE_H = 1
+AT_PROJECT_Q = 2
+AT_GATE = 3
+AT_QUANTISE_Y = 4
+AT_PROJECT_OUT = 5
+
+FLOPS = 2 * 2 * ROWS * D * D
+
+
+def tile_attentionfreetransformerencoder_pb_t_kernel(tc, h, yt, Wq, bq, Wo, bo, out):
+    nc = tc.nc
+
+    h_chunks = h.flatten_outer_dims().rearrange("(c p j) d -> c p (j d)", p=P, j=ROW_TILES)
+    yt_chunks = yt.flatten_outer_dims().rearrange("(c p j) d -> c p (j d)", p=P, j=ROW_TILES)
+    out_chunks = out.flatten_outer_dims().rearrange("(c p j) d -> c p (j d)", p=P, j=ROW_TILES)
+
+    with ExitStack() as ctx:
+        ctx.enter_context(tc.manual_schedule())
+
+        consts = ctx.enter_context(tc.tile_pool(name="consts", bufs=1))
+        rows_in = ctx.enter_context(tc.tile_pool(name="rows_in", bufs=LOOKAHEAD + 1))
+        work = ctx.enter_context(tc.tile_pool(name="work", bufs=3))
+        rows_out = ctx.enter_context(tc.tile_pool(name="rows_out", bufs=4))
+        for_scalar = ctx.enter_context(tc.psum_pool(name="for_scalar", bufs=4))
+        for_vector = ctx.enter_context(tc.psum_pool(name="for_vector", bufs=4))
+
+        def scalar_bank():
+            bank = for_scalar.tile([P, BANK], F32, name="scalar_bank")
+            return bank
+
+        def vector_bank():
+            bank = for_vector.tile([P, BANK], F32, name="vector_bank")
+            return bank
+
+        h_rows = {}
+        yt_rows = {}
+
+        def load_h(c):
+            h_sb = rows_in.tile([P, ROW_TILES * D], BF16, name="h_sb")
+            nc.sync.dma_start(out=h_sb[:], in_=h_chunks[c])
+            h_rows[c] = h_sb
+
+        def load_yt(c):
+            yt_sb = rows_in.tile([P, ROW_TILES * D], BF16, name="yt_sb")
+            nc.sync.dma_start(out=yt_sb[:], in_=yt_chunks[c])
+            yt_rows[c] = yt_sb
+
+        def load_weight(w, name):
+            raw = consts.tile([P, PACK * D], BF16, name=name)
+            nc.sync.dma_start(out=raw[:], in_=w.rearrange("(p t) c -> p (t c)", t=PACK))
+            return raw
+
+        bq_rows = consts.tile([P, D], BF16, name="bq_rows")
+        nc.vector.memset(bq_rows[:], 0.0)
+        nc.scalar.dma_start(out=bq_rows[0:1, :], in_=bq.rearrange("(o d) -> o d", o=1))
+        bo_rows = consts.tile([P, D], BF16, name="bo_rows")
+        nc.vector.memset(bo_rows[:], 0.0)
+        nc.scalar.dma_start(out=bo_rows[0:1, :], in_=bo.rearrange("(o d) -> o d", o=1))
+        ones = consts.tile([P, P], BF16, name="ones")
+        nc.vector.memset(ones[:], 1.0)
+
+        wq_raw = load_weight(Wq, "wq_raw")
+        for c in range(LOOKAHEAD):
+            load_h(c)
+        wo_raw = load_weight(Wo, "wo_raw")
+
+        warm = consts.tile([P, 1], F32, name="warm")
+        nc.vector.memset(warm[:], 0.0)
+        nc.scalar.activation(out=warm[:], in_=warm[:], func=SIGMOID)
+
+        ident = consts.tile([P, P], F32, name="ident")
+        make_identity(nc, ident[:])
+
+        wq_grouped = consts.tile([P, D * PACK], BF16, name="wq_grouped", align_bytes=64)
+        wq_from = wq_raw[:].rearrange("p (t q m) -> p m q t", t=PACK, m=PACK)
+        wq_to = wq_grouped[:].rearrange("p (m q t) -> p m q t", m=PACK, t=PACK)
+        for m in range(PACK):
+            nc.vector.tensor_copy(out=wq_to[:, m], in_=wq_from[:, m])
+        wq_codes = consts.tile([P, D], U32, name="wq_codes", align_bytes=64)
+        wq_scales = consts.tile([P, D], U8, name="wq_scales", align_bytes=64)
+        nc.vector.quantize_mx(out=wq_codes[:].bitcast(FP8X4), scales=wq_scales[:], in_=wq_grouped[:])
+
+        bq_cols = consts.tile([P, PACK], F32, name="bq_cols")
+
+        def stand_bq_up():
+            bq_ps = vector_bank()
+            for u in range(2):
+                nc.tensor.transpose(
+                    bq_ps[:, u * P : (u + 1) * P], bq_rows[:].bitcast(F32)[:, u::2], ident[:]
+                )
+            nc.vector.tensor_copy(
+                out=bq_cols[:].rearrange("p (u e) -> p u e", u=2),
+                in_=bq_ps[:, 0 : 2 * P].bitcast(BF16).rearrange("p (u x) -> p u x", u=2)[:, :, 0:2],
+            )
+
+        wo_codes = consts.tile([P, D], U32, name="wo_codes", align_bytes=64)
+        wo_scales = consts.tile([P, D], U8, name="wo_scales", align_bytes=64)
+        bo_all = consts.tile([P, D], F32, name="bo_all")
+
+        def prepare_second_product():
+            wo_grouped = consts.tile([P, D * PACK], BF16, name="wo_grouped", align_bytes=64)
+            nc.vector.tensor_copy(
+                out=wo_grouped[:].rearrange("p (c t) -> p c t", t=PACK),
+                in_=wo_raw[:].rearrange("p (t c) -> p c t", t=PACK),
+            )
+            bo_ps = vector_bank()
+            nc.tensor.matmul(out=bo_ps[:], lhsT=ones[:], rhs=bo_rows[:], start=True, stop=True)
+            nc.vector.tensor_copy(out=bo_all[:], in_=bo_ps[:])
+            nc.vector.quantize_mx(
+                out=wo_codes[:].bitcast(FP8X4), scales=wo_scales[:], in_=wo_grouped[:]
+            )
+
+        def transpose_words(bank, rows_sb, half):
+            words = rows_sb[:].bitcast(F32)
+            for j in range(2):
+                first = (2 * half + j) * (D // 2)
+                for u in range(2):
+                    nc.tensor.transpose(
+                        bank[:, u * HALF + j * P : u * HALF + (j + 1) * P],
+                        words[:, first + u : first + D // 2 : 2],
+                        ident[:],
+                    )
+
+        h_grouped = {}
+        h_mx = {}
+        yt_banks = {}
+        gates = {}
+        y_grouped = {}
+        y_mx = {}
+        out_rows = {}
+
+        def transpose_h(c, half):
+            if half == 0:
+                grouped = work.tile([P, CHUNK * PACK], BF16, name="h_grouped", align_bytes=64)
+                h_grouped[c] = grouped
+            bank = scalar_bank()
+            transpose_words(bank, h_rows[c], half)
+            nc.scalar.copy(
+                out=h_grouped[c][:]
+                .bitcast(F32)[:, half * BANK : (half + 1) * BANK]
+                .rearrange("p (r u) -> p r u", u=2),
+                in_=bank[:].rearrange("p (u r) -> p r u", u=2),
+            )
+
+        def quantise_h(c):
+            codes = work.tile([P, CHUNK], U32, name="h_codes", align_bytes=64)
+            scales = work.tile([P, CHUNK], U8, name="h_scales", align_bytes=64)
+            nc.vector.quantize_mx(out=codes[:].bitcast(FP8X4), scales=scales[:], in_=h_grouped[c][:])
+            h_mx[c] = (codes, scales)
+
+        def project_q(c, m):
+            if m == 0:
+                gate = work.tile([P, PACK * CHUNK], F32, name="gate")
+                gates[c] = gate
+            codes, scales = h_mx[c]
+            q_ps = scalar_bank()
+            nc.tensor.matmul_mx(
+                out=q_ps[:],
+                lhsT=wq_codes[:, m * P : (m + 1) * P].bitcast(FP8X4),
+                lhsT_scale=wq_scales[:, m * P : (m + 1) * P],
+                rhs=codes[:].bitcast(FP8X4),
+                rhs_scale=scales[:],
+                start=True,
+                stop=True,
+            )
+            nc.scalar.activation(
+                out=gates[c][:, m * CHUNK : (m + 1) * CHUNK],
+                in_=q_ps[:],
+                func=SIGMOID,
+                bias=bq_cols[:, m : m + 1],
+                scale=1.0,
+            )
+
+        def transpose_yt(c, half):
+            bank = vector_bank()
+            transpose_words(bank, yt_rows[c], half)
+            yt_banks[(c, half)] = bank
+
+        def apply_gate(c, half):
+            if half == 0:
+                grouped = work.tile([P, CHUNK * PACK], BF16, name="y_grouped", align_bytes=64)
+                y_grouped[c] = grouped
+            nc.vector.tensor_tensor(
+                out=y_grouped[c][:, half * HALF * PACK : (half + 1) * HALF * PACK].rearrange(
+                    "p (r u e) -> p r u e", u=2, e=2
+                ),
+                in0=gates[c][:].rearrange("p (u e r) -> p r u e", u=2, e=2)[
+                    :, half * HALF : (half + 1) * HALF
+                ],
+                in1=yt_banks[(c, half)][:].bitcast(BF16).rearrange("p (u r e) -> p r u e", u=2, e=2),
+                op=MULT,
+            )
+
+        def quantise_y(c):
+            codes = work.tile([P, CHUNK], U32, name="y_codes", align_bytes=64)
+            scales = work.tile([P, CHUNK], U8, name="y_scales", align_bytes=64)
+            nc.vector.quantize_mx(out=codes[:].bitcast(FP8X4), scales=scales[:], in_=y_grouped[c][:])
+            y_mx[c] = (codes, scales)
+
+        def project_out(c, j):
+            if j == 0:
+                o_sb = rows_out.tile([P, ROW_TILES * D], F32, name="o_sb")
+                out_rows[c] = o_sb
+            codes, scales = y_mx[c]
+            through_vector = j % 2 == 0 or c == CHUNKS - 1
+            o_ps = vector_bank() if through_vector else scalar_bank()
+            nc.tensor.matmul_mx(
+                out=o_ps[:],
+                lhsT=codes[:, j * P : (j + 1) * P].bitcast(FP8X4),
+                lhsT_scale=scales[:, j * P : (j + 1) * P],
+                rhs=wo_codes[:].bitcast(FP8X4),
+                rhs_scale=wo_scales[:],
+                start=True,
+                stop=True,
+            )
+            dest = out_rows[c][:, j * D : (j + 1) * D]
+            if through_vector:
+                nc.vector.tensor_tensor(out=dest, in0=o_ps[:], in1=bo_all[:], op=ADD)
+            else:
+                nc.scalar.copy(out=dest, in_=o_ps[:])
+                nc.gpsimd.tensor_tensor(out=dest, in0=dest, in1=bo_all[:], op=ADD)
+            if j % 2 == 1:
+                pair = slice((j - 1) * D, (j + 1) * D)
+                nc.sync.dma_start(out=out_chunks[c][:, pair], in_=out_rows[c][:, pair])
+
+        def live(c):
+            return 0 <= c < CHUNKS
+
+        for s in range(CHUNKS + AT_PROJECT_OUT):
+            if live(s + LOOKAHEAD):
+                load_h(s + LOOKAHEAD)
+            if live(s - AT_GATE + LOOKAHEAD):
+                load_yt(s - AT_GATE + LOOKAHEAD)
+            if live(s - AT_QUANTISE_Y):
+                quantise_y(s - AT_QUANTISE_Y)
+            if live(s - AT_QUANTISE_H):
+                quantise_h(s - AT_QUANTISE_H)
+            if s == AT_PROJECT_Q - 1:
+                stand_bq_up()
+            if s == AT_PROJECT_Q:
+                prepare_second_product()
+            for half in range(2):
+                if live(s - AT_GATE):
+                    transpose_yt(s - AT_GATE, half)
+                    apply_gate(s - AT_GATE, half)
+                if live(s):
+                    transpose_h(s, half)
+                for k in (2 * half, 2 * half + 1):
+                    if live(s - AT_PROJECT_Q):
+                        project_q(s - AT_PROJECT_Q, k)
+                    if live(s - AT_PROJECT_OUT):
+                        project_out(s - AT_PROJECT_OUT, k)

@@ -20,6 +20,7 @@ CHUNK = 512
 CHUNKS = ROWS // CHUNK
 ROW_TILES = CHUNK // P
 HALF = CHUNK // 2
+LINE = 4
 BANK = 512
 LOOKAHEAD = 3
 
@@ -135,15 +136,13 @@ def tile_attentionfreetransformerencoder_pb_t_kernel(tc, h, yt, Wq, bq, Wo, bo, 
                 out=wo_codes[:].bitcast(FP8X4), scales=wo_scales[:], in_=wo_grouped[:]
             )
 
-        def transpose_words(bank, rows_sb, half):
+        def transpose_words(planes, rows_sb, half):
             words = rows_sb[:].bitcast(F32)
             for j in range(2):
                 first = (2 * half + j) * (D // 2)
                 for u in range(2):
                     nc.tensor.transpose(
-                        bank[:, u * HALF + j * P : u * HALF + (j + 1) * P],
-                        words[:, first + u : first + D // 2 : 2],
-                        ident[:],
+                        planes[u][j], words[:, first + u : first + D // 2 : 2], ident[:]
                     )
 
         h_grouped = {}
@@ -159,7 +158,8 @@ def tile_attentionfreetransformerencoder_pb_t_kernel(tc, h, yt, Wq, bq, Wo, bo, 
                 grouped = work.tile([P, CHUNK * PACK], BF16, name="h_grouped", align_bytes=64)
                 h_grouped[c] = grouped
             bank = scalar_bank()
-            transpose_words(bank, h_rows[c], half)
+            plane = bank[:].rearrange("p (u j r) -> p u j r", u=2, j=2)
+            transpose_words([[plane[:, u, j] for j in range(2)] for u in range(2)], h_rows[c], half)
             nc.scalar.copy(
                 out=h_grouped[c][:]
                 .bitcast(F32)[:, half * BANK : (half + 1) * BANK]
@@ -198,7 +198,8 @@ def tile_attentionfreetransformerencoder_pb_t_kernel(tc, h, yt, Wq, bq, Wo, bo, 
 
         def transpose_yt(c, half):
             bank = vector_bank()
-            transpose_words(bank, yt_rows[c], half)
+            plane = bank[:].rearrange("p (j c u i) -> p u j c i", j=2, u=2, i=LINE)
+            transpose_words([[plane[:, u, j] for j in range(2)] for u in range(2)], yt_rows[c], half)
             yt_banks[(c, half)] = bank
 
         def apply_gate(c, half):
@@ -207,12 +208,14 @@ def tile_attentionfreetransformerencoder_pb_t_kernel(tc, h, yt, Wq, bq, Wo, bo, 
                 y_grouped[c] = grouped
             nc.vector.tensor_tensor(
                 out=y_grouped[c][:, half * HALF * PACK : (half + 1) * HALF * PACK].rearrange(
-                    "p (r u e) -> p r u e", u=2, e=2
+                    "p (c i u e) -> p c u e i", i=LINE, u=2, e=2
                 ),
-                in0=gates[c][:].rearrange("p (u e r) -> p r u e", u=2, e=2)[
-                    :, half * HALF : (half + 1) * HALF
+                in0=gates[c][:].rearrange("p (u e c i) -> p c u e i", u=2, e=2, i=LINE)[
+                    :, half * (HALF // LINE) : (half + 1) * (HALF // LINE)
                 ],
-                in1=yt_banks[(c, half)][:].bitcast(BF16).rearrange("p (u r e) -> p r u e", u=2, e=2),
+                in1=yt_banks[(c, half)][:].bitcast(BF16).rearrange(
+                    "p (c u i e) -> p c u e i", u=2, i=LINE, e=2
+                ),
                 op=MULT,
             )
 

@@ -16,13 +16,15 @@ ROWS = 8 * 1024
 D = 512
 P = 128
 PACK = 4
-CHUNK = 512
-CHUNKS = ROWS // CHUNK
-ROW_TILES = CHUNK // P
-HALF = CHUNK // 2
+CHUNK_TILES = (1, 1, 2) + (4,) * 14 + (2, 1, 1)
+CHUNKS = len(CHUNK_TILES)
+FIRST_TILE = tuple(sum(CHUNK_TILES[:c]) for c in range(CHUNKS))
+ROW_TILES = ROWS // P
+MAX_TILES = max(CHUNK_TILES)
+UNIT_TILES = 2
 LINE = 4
 BANK = 512
-LOOKAHEAD = 3
+LOOKAHEAD = 6
 
 AT_QUANTISE_H = 1
 AT_PROJECT_Q = 2
@@ -36,9 +38,10 @@ FLOPS = 2 * 2 * ROWS * D * D
 def tile_attentionfreetransformerencoder_pb_t_kernel(tc, h, yt, Wq, bq, Wo, bo, out):
     nc = tc.nc
 
-    h_chunks = h.flatten_outer_dims().rearrange("(c p j) d -> c p (j d)", p=P, j=ROW_TILES)
-    yt_chunks = yt.flatten_outer_dims().rearrange("(c p j) d -> c p (j d)", p=P, j=ROW_TILES)
-    out_chunks = out.flatten_outer_dims().rearrange("(c p j) d -> c p (j d)", p=P, j=ROW_TILES)
+    def chunk_rows(dram, c):
+        first = FIRST_TILE[c] * P
+        rows = dram.flatten_outer_dims()[first : first + CHUNK_TILES[c] * P, :]
+        return rows.rearrange("(p j) d -> p (j d)", p=P)
 
     with ExitStack() as ctx:
         ctx.enter_context(tc.manual_schedule())
@@ -62,13 +65,13 @@ def tile_attentionfreetransformerencoder_pb_t_kernel(tc, h, yt, Wq, bq, Wo, bo, 
         yt_rows = {}
 
         def load_h(c):
-            h_sb = rows_in.tile([P, ROW_TILES * D], BF16, name="h_sb")
-            nc.sync.dma_start(out=h_sb[:], in_=h_chunks[c])
+            h_sb = rows_in.tile([P, MAX_TILES * D], BF16, name="h_sb")
+            nc.sync.dma_start(out=h_sb[:, : CHUNK_TILES[c] * D], in_=chunk_rows(h, c))
             h_rows[c] = h_sb
 
         def load_yt(c):
-            yt_sb = rows_in.tile([P, ROW_TILES * D], BF16, name="yt_sb")
-            nc.sync.dma_start(out=yt_sb[:], in_=yt_chunks[c])
+            yt_sb = rows_in.tile([P, MAX_TILES * D], BF16, name="yt_sb")
+            nc.sync.dma_start(out=yt_sb[:, : CHUNK_TILES[c] * D], in_=chunk_rows(yt, c))
             yt_rows[c] = yt_sb
 
         def load_weight(w, name):
@@ -76,26 +79,29 @@ def tile_attentionfreetransformerencoder_pb_t_kernel(tc, h, yt, Wq, bq, Wo, bo, 
             nc.sync.dma_start(out=raw[:], in_=w.rearrange("(p t) c -> p (t c)", t=PACK))
             return raw
 
-        bq_rows = consts.tile([P, D], BF16, name="bq_rows")
-        nc.vector.memset(bq_rows[:], 0.0)
-        nc.scalar.dma_start(out=bq_rows[0:1, :], in_=bq.rearrange("(o d) -> o d", o=1))
-        bo_rows = consts.tile([P, D], BF16, name="bo_rows")
-        nc.vector.memset(bo_rows[:], 0.0)
-        nc.scalar.dma_start(out=bo_rows[0:1, :], in_=bo.rearrange("(o d) -> o d", o=1))
-        ones = consts.tile([P, P], BF16, name="ones")
-        nc.vector.memset(ones[:], 1.0)
-
-        wq_raw = load_weight(Wq, "wq_raw")
-        for c in range(LOOKAHEAD):
-            load_h(c)
-        wo_raw = load_weight(Wo, "wo_raw")
-
         warm = consts.tile([P, 1], F32, name="warm")
         nc.vector.memset(warm[:], 0.0)
         nc.scalar.activation(out=warm[:], in_=warm[:], func=SIGMOID)
 
         ident = consts.tile([P, P], F32, name="ident")
         make_identity(nc, ident[:])
+        bo_rows = consts.tile([P, D], BF16, name="bo_rows")
+        nc.gpsimd.memset(bo_rows[:], 0.0)
+        ones = consts.tile([P, P], BF16, name="ones")
+        nc.gpsimd.memset(ones[:], 1.0)
+
+        wq_raw = load_weight(Wq, "wq_raw")
+        load_h(0)
+        bq_cols = consts.tile([P, PACK], BF16, name="bq_cols")
+        nc.sync.dma_start(out=bq_cols[:], in_=bq.rearrange("(p m) -> p m", m=PACK))
+        for c in range(1, AT_GATE):
+            load_h(c)
+        for s in range(AT_GATE, LOOKAHEAD):
+            load_yt(s - AT_GATE)
+            load_h(s)
+            if s == AT_GATE:
+                wo_raw = load_weight(Wo, "wo_raw")
+                nc.sync.dma_start(out=bo_rows[0:1, :], in_=bo.rearrange("(o d) -> o d", o=1))
 
         wq_grouped = consts.tile([P, D * PACK], BF16, name="wq_grouped", align_bytes=64)
         wq_from = wq_raw[:].rearrange("p (t q m) -> p m q t", t=PACK, m=PACK)
@@ -106,40 +112,33 @@ def tile_attentionfreetransformerencoder_pb_t_kernel(tc, h, yt, Wq, bq, Wo, bo, 
         wq_scales = consts.tile([P, D], U8, name="wq_scales", align_bytes=64)
         nc.vector.quantize_mx(out=wq_codes[:].bitcast(FP8X4), scales=wq_scales[:], in_=wq_grouped[:])
 
-        bq_cols = consts.tile([P, PACK], F32, name="bq_cols")
-
-        def stand_bq_up():
-            bq_ps = vector_bank()
-            for u in range(2):
-                nc.tensor.transpose(
-                    bq_ps[:, u * P : (u + 1) * P], bq_rows[:].bitcast(F32)[:, u::2], ident[:]
-                )
-            nc.vector.tensor_copy(
-                out=bq_cols[:].rearrange("p (u e) -> p u e", u=2),
-                in_=bq_ps[:, 0 : 2 * P].bitcast(BF16).rearrange("p (u x) -> p u x", u=2)[:, :, 0:2],
-            )
-
+        wo_grouped = consts.tile([P, D * PACK], BF16, name="wo_grouped", align_bytes=64)
         wo_codes = consts.tile([P, D], U32, name="wo_codes", align_bytes=64)
         wo_scales = consts.tile([P, D], U8, name="wo_scales", align_bytes=64)
         bo_all = consts.tile([P, D], F32, name="bo_all")
 
-        def prepare_second_product():
-            wo_grouped = consts.tile([P, D * PACK], BF16, name="wo_grouped", align_bytes=64)
+        def group_wo():
             nc.vector.tensor_copy(
                 out=wo_grouped[:].rearrange("p (c t) -> p c t", t=PACK),
                 in_=wo_raw[:].rearrange("p (t c) -> p c t", t=PACK),
             )
-            bo_ps = vector_bank()
-            nc.tensor.matmul(out=bo_ps[:], lhsT=ones[:], rhs=bo_rows[:], start=True, stop=True)
-            nc.vector.tensor_copy(out=bo_all[:], in_=bo_ps[:])
+
+        def quantise_wo():
             nc.vector.quantize_mx(
                 out=wo_codes[:].bitcast(FP8X4), scales=wo_scales[:], in_=wo_grouped[:]
             )
+            bo_ps = vector_bank()
+            nc.tensor.matmul(out=bo_ps[:], lhsT=ones[:], rhs=bo_rows[:], start=True, stop=True)
+            nc.vector.tensor_copy(out=bo_all[:], in_=bo_ps[:])
 
-        def transpose_words(planes, rows_sb, half):
+        def units(c):
+            tiles = CHUNK_TILES[c]
+            return [(j, min(UNIT_TILES, tiles - j)) for j in range(0, tiles, UNIT_TILES)]
+
+        def transpose_words(planes, rows_sb, first_tile):
             words = rows_sb[:].bitcast(F32)
-            for j in range(2):
-                first = (2 * half + j) * (D // 2)
+            for j in range(len(planes[0])):
+                first = (first_tile + j) * (D // 2)
                 for u in range(2):
                     nc.tensor.transpose(
                         planes[u][j], words[:, first + u : first + D // 2 : 2], ident[:]
@@ -153,84 +152,97 @@ def tile_attentionfreetransformerencoder_pb_t_kernel(tc, h, yt, Wq, bq, Wo, bo, 
         y_mx = {}
         out_rows = {}
 
-        def transpose_h(c, half):
-            if half == 0:
-                grouped = work.tile([P, CHUNK * PACK], BF16, name="h_grouped", align_bytes=64)
+        def transpose_h(c, first_tile, tiles):
+            if first_tile == 0:
+                grouped = work.tile([P, MAX_TILES * P * PACK], BF16, name="h_grouped", align_bytes=64)
                 h_grouped[c] = grouped
+            words = tiles * 2 * P
             bank = scalar_bank()
-            plane = bank[:].rearrange("p (u j r) -> p u j r", u=2, j=2)
-            transpose_words([[plane[:, u, j] for j in range(2)] for u in range(2)], h_rows[c], half)
+            plane = bank[:, :words].rearrange("p (u j r) -> p u j r", u=2, j=tiles)
+            transpose_words([[plane[:, u, j] for j in range(tiles)] for u in range(2)], h_rows[c], first_tile)
+            start = first_tile * 2 * P
             nc.scalar.copy(
                 out=h_grouped[c][:]
-                .bitcast(F32)[:, half * BANK : (half + 1) * BANK]
+                .bitcast(F32)[:, start : start + words]
                 .rearrange("p (r u) -> p r u", u=2),
-                in_=bank[:].rearrange("p (u r) -> p r u", u=2),
+                in_=bank[:, :words].rearrange("p (u r) -> p r u", u=2),
             )
 
+        def quantise(grouped, c, names):
+            rows = CHUNK_TILES[c] * P
+            codes = work.tile([P, MAX_TILES * P], U32, name=names[0], align_bytes=64)
+            scales = work.tile([P, MAX_TILES * P], U8, name=names[1], align_bytes=64)
+            nc.vector.quantize_mx(
+                out=codes[:, :rows].bitcast(FP8X4),
+                scales=scales[:, :rows],
+                in_=grouped[:, : rows * PACK],
+            )
+            return codes, scales
+
         def quantise_h(c):
-            codes = work.tile([P, CHUNK], U32, name="h_codes", align_bytes=64)
-            scales = work.tile([P, CHUNK], U8, name="h_scales", align_bytes=64)
-            nc.vector.quantize_mx(out=codes[:].bitcast(FP8X4), scales=scales[:], in_=h_grouped[c][:])
-            h_mx[c] = (codes, scales)
+            h_mx[c] = quantise(h_grouped[c], c, ("h_codes", "h_scales"))
 
         def project_q(c, m):
+            rows = CHUNK_TILES[c] * P
             if m == 0:
-                gate = work.tile([P, PACK * CHUNK], F32, name="gate")
+                gate = work.tile([P, PACK * MAX_TILES * P], F32, name="gate")
                 gates[c] = gate
             codes, scales = h_mx[c]
             q_ps = scalar_bank()
             nc.tensor.matmul_mx(
-                out=q_ps[:],
+                out=q_ps[:, :rows],
                 lhsT=wq_codes[:, m * P : (m + 1) * P].bitcast(FP8X4),
                 lhsT_scale=wq_scales[:, m * P : (m + 1) * P],
-                rhs=codes[:].bitcast(FP8X4),
-                rhs_scale=scales[:],
+                rhs=codes[:, :rows].bitcast(FP8X4),
+                rhs_scale=scales[:, :rows],
                 start=True,
                 stop=True,
             )
             nc.scalar.activation(
-                out=gates[c][:, m * CHUNK : (m + 1) * CHUNK],
-                in_=q_ps[:],
+                out=gates[c][:, m * rows : (m + 1) * rows],
+                in_=q_ps[:, :rows],
                 func=SIGMOID,
                 bias=bq_cols[:, m : m + 1],
                 scale=1.0,
             )
 
-        def transpose_yt(c, half):
+        def transpose_yt(c, first_tile, tiles):
             bank = vector_bank()
-            plane = bank[:].rearrange("p (j c u i) -> p u j c i", j=2, u=2, i=LINE)
-            transpose_words([[plane[:, u, j] for j in range(2)] for u in range(2)], yt_rows[c], half)
-            yt_banks[(c, half)] = bank
+            plane = bank[:, : tiles * 2 * P].rearrange(
+                "p (j c u i) -> p u j c i", j=tiles, u=2, i=LINE
+            )
+            transpose_words([[plane[:, u, j] for j in range(tiles)] for u in range(2)], yt_rows[c], first_tile)
+            yt_banks[(c, first_tile)] = bank
 
-        def apply_gate(c, half):
-            if half == 0:
-                grouped = work.tile([P, CHUNK * PACK], BF16, name="y_grouped", align_bytes=64)
+        def apply_gate(c, first_tile, tiles):
+            if first_tile == 0:
+                grouped = work.tile([P, MAX_TILES * P * PACK], BF16, name="y_grouped", align_bytes=64)
                 y_grouped[c] = grouped
+            chunk = CHUNK_TILES[c] * P
+            first, rows = first_tile * P, tiles * P
             nc.vector.tensor_tensor(
-                out=y_grouped[c][:, half * HALF * PACK : (half + 1) * HALF * PACK].rearrange(
+                out=y_grouped[c][:, first * PACK : (first + rows) * PACK].rearrange(
                     "p (c i u e) -> p c u e i", i=LINE, u=2, e=2
                 ),
-                in0=gates[c][:].rearrange("p (u e c i) -> p c u e i", u=2, e=2, i=LINE)[
-                    :, half * (HALF // LINE) : (half + 1) * (HALF // LINE)
-                ],
-                in1=yt_banks[(c, half)][:].bitcast(BF16).rearrange(
-                    "p (c u i e) -> p c u e i", u=2, i=LINE, e=2
-                ),
+                in0=gates[c][:, : PACK * chunk].rearrange(
+                    "p (u e c i) -> p c u e i", u=2, e=2, i=LINE
+                )[:, first // LINE : (first + rows) // LINE],
+                in1=yt_banks[(c, first_tile)][:, : 2 * rows]
+                .bitcast(BF16)
+                .rearrange("p (c u i e) -> p c u e i", u=2, i=LINE, e=2),
                 op=MULT,
             )
 
         def quantise_y(c):
-            codes = work.tile([P, CHUNK], U32, name="y_codes", align_bytes=64)
-            scales = work.tile([P, CHUNK], U8, name="y_scales", align_bytes=64)
-            nc.vector.quantize_mx(out=codes[:].bitcast(FP8X4), scales=scales[:], in_=y_grouped[c][:])
-            y_mx[c] = (codes, scales)
+            y_mx[c] = quantise(y_grouped[c], c, ("y_codes", "y_scales"))
 
         def project_out(c, j):
             if j == 0:
-                o_sb = rows_out.tile([P, ROW_TILES * D], F32, name="o_sb")
+                o_sb = rows_out.tile([P, MAX_TILES * D], F32, name="o_sb")
                 out_rows[c] = o_sb
             codes, scales = y_mx[c]
-            through_vector = j % 2 == 0 or c == CHUNKS - 1
+            tile_index = FIRST_TILE[c] + j
+            through_vector = (tile_index % 2 == 0) != (tile_index >= ROW_TILES - 2)
             o_ps = vector_bank() if through_vector else scalar_bank()
             nc.tensor.matmul_mx(
                 out=o_ps[:],
@@ -247,9 +259,9 @@ def tile_attentionfreetransformerencoder_pb_t_kernel(tc, h, yt, Wq, bq, Wo, bo, 
             else:
                 nc.scalar.copy(out=dest, in_=o_ps[:])
                 nc.gpsimd.tensor_tensor(out=dest, in0=dest, in1=bo_all[:], op=ADD)
-            if j % 2 == 1:
-                pair = slice((j - 1) * D, (j + 1) * D)
-                nc.sync.dma_start(out=out_chunks[c][:, pair], in_=out_rows[c][:, pair])
+            if j % 2 == 1 or CHUNK_TILES[c] == 1:
+                done = slice((j // 2) * 2 * D, (j + 1) * D)
+                nc.sync.dma_start(out=chunk_rows(out, c)[:, done], in_=out_rows[c][:, done])
 
         def live(c):
             return 0 <= c < CHUNKS
@@ -263,18 +275,18 @@ def tile_attentionfreetransformerencoder_pb_t_kernel(tc, h, yt, Wq, bq, Wo, bo, 
                 quantise_y(s - AT_QUANTISE_Y)
             if live(s - AT_QUANTISE_H):
                 quantise_h(s - AT_QUANTISE_H)
-            if s == AT_PROJECT_Q - 1:
-                stand_bq_up()
-            if s == AT_PROJECT_Q:
-                prepare_second_product()
             for half in range(2):
-                if live(s - AT_GATE):
-                    transpose_yt(s - AT_GATE, half)
-                    apply_gate(s - AT_GATE, half)
-                if live(s):
-                    transpose_h(s, half)
+                if live(s - AT_GATE) and half < len(units(s - AT_GATE)):
+                    transpose_yt(s - AT_GATE, *units(s - AT_GATE)[half])
+                    apply_gate(s - AT_GATE, *units(s - AT_GATE)[half])
+                if live(s) and half < len(units(s)):
+                    transpose_h(s, *units(s)[half])
                 for k in (2 * half, 2 * half + 1):
                     if live(s - AT_PROJECT_Q):
                         project_q(s - AT_PROJECT_Q, k)
-                    if live(s - AT_PROJECT_OUT):
+                    if live(s - AT_PROJECT_OUT) and k < CHUNK_TILES[s - AT_PROJECT_OUT]:
                         project_out(s - AT_PROJECT_OUT, k)
+            if s == AT_GATE:
+                group_wo()
+            if s == AT_GATE + 1:
+                quantise_wo()

@@ -26,11 +26,9 @@ LINE = 4
 BANK = 512
 LOOKAHEAD = 6
 
-AT_QUANTISE_H = 1
-AT_PROJECT_Q = 2
-AT_GATE = 3
-AT_QUANTISE_Y = 4
-AT_PROJECT_OUT = 5
+AT_PROJECT_Q = 1
+AT_GATE = 2
+AT_PROJECT_OUT = 3
 
 FLOPS = 2 * 2 * ROWS * D * D
 
@@ -271,22 +269,23 @@ def tile_attentionfreetransformerencoder_pb_t_kernel(tc, h, yt, Wq, bq, Wo, bo, 
                 load_h(s + LOOKAHEAD)
             if live(s - AT_GATE + LOOKAHEAD):
                 load_yt(s - AT_GATE + LOOKAHEAD)
-            if live(s - AT_QUANTISE_Y):
-                quantise_y(s - AT_QUANTISE_Y)
-            if live(s - AT_QUANTISE_H):
-                quantise_h(s - AT_QUANTISE_H)
             for half in range(2):
                 if live(s - AT_GATE) and half < len(units(s - AT_GATE)):
                     transpose_yt(s - AT_GATE, *units(s - AT_GATE)[half])
                     apply_gate(s - AT_GATE, *units(s - AT_GATE)[half])
                 if live(s) and half < len(units(s)):
                     transpose_h(s, *units(s)[half])
-                for k in (2 * half, 2 * half + 1):
-                    if live(s - AT_PROJECT_Q):
-                        project_q(s - AT_PROJECT_Q, k)
-                    if live(s - AT_PROJECT_OUT) and k < CHUNK_TILES[s - AT_PROJECT_OUT]:
-                        project_out(s - AT_PROJECT_OUT, k)
-            if s == AT_GATE:
+            if live(s):
+                quantise_h(s)
+            if live(s - AT_GATE):
+                quantise_y(s - AT_GATE)
+            if live(s - AT_PROJECT_Q):
+                for m in range(PACK):
+                    project_q(s - AT_PROJECT_Q, m)
+            if live(s - AT_PROJECT_OUT):
+                for j in range(CHUNK_TILES[s - AT_PROJECT_OUT]):
+                    project_out(s - AT_PROJECT_OUT, j)
+            if s == AT_PROJECT_Q:
                 group_wo()
-            if s == AT_GATE + 1:
+            if s == AT_GATE:
                 quantise_wo()

@@ -16,7 +16,7 @@ ROWS = 8 * 1024
 D = 512
 P = 128
 PACK = 4
-CHUNK_TILES = (1, 1, 2) + (4,) * 14 + (2, 1, 1)
+CHUNK_TILES = (2,) + (4,) * 15 + (2,)
 CHUNKS = len(CHUNK_TILES)
 FIRST_TILE = tuple(sum(CHUNK_TILES[:c]) for c in range(CHUNKS))
 ROW_TILES = ROWS // P
@@ -48,8 +48,8 @@ def tile_attentionfreetransformerencoder_pb_t_kernel(tc, h, yt, Wq, bq, Wo, bo, 
         rows_in = ctx.enter_context(tc.tile_pool(name="rows_in", bufs=LOOKAHEAD + 1))
         work = ctx.enter_context(tc.tile_pool(name="work", bufs=3))
         rows_out = ctx.enter_context(tc.tile_pool(name="rows_out", bufs=4))
-        for_scalar = ctx.enter_context(tc.psum_pool(name="for_scalar", bufs=4))
-        for_vector = ctx.enter_context(tc.psum_pool(name="for_vector", bufs=4))
+        for_scalar = ctx.enter_context(tc.psum_pool(name="for_scalar", bufs=5))
+        for_vector = ctx.enter_context(tc.psum_pool(name="for_vector", bufs=3))
 
         def scalar_bank():
             bank = for_scalar.tile([P, BANK], F32, name="scalar_bank")
@@ -277,13 +277,15 @@ def tile_attentionfreetransformerencoder_pb_t_kernel(tc, h, yt, Wq, bq, Wo, bo, 
                     transpose_h(s, *units(s)[half])
             if live(s):
                 quantise_h(s)
-            if live(s - AT_GATE):
-                quantise_y(s - AT_GATE)
             if live(s - AT_PROJECT_Q):
                 for m in range(PACK):
                     project_q(s - AT_PROJECT_Q, m)
             if live(s - AT_PROJECT_OUT):
-                for j in range(CHUNK_TILES[s - AT_PROJECT_OUT]):
+                project_out(s - AT_PROJECT_OUT, 0)
+            if live(s - AT_GATE):
+                quantise_y(s - AT_GATE)
+            if live(s - AT_PROJECT_OUT):
+                for j in range(1, CHUNK_TILES[s - AT_PROJECT_OUT]):
                     project_out(s - AT_PROJECT_OUT, j)
             if s == AT_PROJECT_Q:
                 group_wo()

@@ -24,6 +24,7 @@ MAX_TILES = max(CHUNK_TILES)
 UNIT_TILES = 2
 LINE = 4
 BANK = 512
+MX_ALIGN = 256
 LOOKAHEAD = 6
 
 AT_PROJECT_Q = 1
@@ -101,18 +102,18 @@ def tile_attentionfreetransformerencoder_pb_t_kernel(tc, h, yt, Wq, bq, Wo, bo, 
                 wo_raw = load_weight(Wo, "wo_raw")
                 nc.sync.dma_start(out=bo_rows[0:1, :], in_=bo.rearrange("(o d) -> o d", o=1))
 
-        wq_grouped = consts.tile([P, D * PACK], BF16, name="wq_grouped", align_bytes=64)
+        wq_grouped = consts.tile([P, D * PACK], BF16, name="wq_grouped", align_bytes=MX_ALIGN)
         wq_from = wq_raw[:].rearrange("p (t q m) -> p m q t", t=PACK, m=PACK)
         wq_to = wq_grouped[:].rearrange("p (m q t) -> p m q t", m=PACK, t=PACK)
         for m in range(PACK):
             nc.vector.tensor_copy(out=wq_to[:, m], in_=wq_from[:, m])
-        wq_codes = consts.tile([P, D], U32, name="wq_codes", align_bytes=64)
-        wq_scales = consts.tile([P, D], U8, name="wq_scales", align_bytes=64)
+        wq_codes = consts.tile([P, D], U32, name="wq_codes", align_bytes=MX_ALIGN)
+        wq_scales = consts.tile([P, D], U8, name="wq_scales", align_bytes=MX_ALIGN)
         nc.vector.quantize_mx(out=wq_codes[:].bitcast(FP8X4), scales=wq_scales[:], in_=wq_grouped[:])
 
-        wo_grouped = consts.tile([P, D * PACK], BF16, name="wo_grouped", align_bytes=64)
-        wo_codes = consts.tile([P, D], U32, name="wo_codes", align_bytes=64)
-        wo_scales = consts.tile([P, D], U8, name="wo_scales", align_bytes=64)
+        wo_grouped = consts.tile([P, D * PACK], BF16, name="wo_grouped", align_bytes=MX_ALIGN)
+        wo_codes = consts.tile([P, D], U32, name="wo_codes", align_bytes=MX_ALIGN)
+        wo_scales = consts.tile([P, D], U8, name="wo_scales", align_bytes=MX_ALIGN)
         bo_all = consts.tile([P, D], F32, name="bo_all")
 
         def group_wo():
@@ -152,7 +153,7 @@ def tile_attentionfreetransformerencoder_pb_t_kernel(tc, h, yt, Wq, bq, Wo, bo, 
 
         def transpose_h(c, first_tile, tiles):
             if first_tile == 0:
-                grouped = work.tile([P, MAX_TILES * P * PACK], BF16, name="h_grouped", align_bytes=64)
+                grouped = work.tile([P, MAX_TILES * P * PACK], BF16, name="h_grouped", align_bytes=MX_ALIGN)
                 h_grouped[c] = grouped
             words = tiles * 2 * P
             bank = scalar_bank()
@@ -168,8 +169,8 @@ def tile_attentionfreetransformerencoder_pb_t_kernel(tc, h, yt, Wq, bq, Wo, bo, 
 
         def quantise(grouped, c, names):
             rows = CHUNK_TILES[c] * P
-            codes = work.tile([P, MAX_TILES * P], U32, name=names[0], align_bytes=64)
-            scales = work.tile([P, MAX_TILES * P], U8, name=names[1], align_bytes=64)
+            codes = work.tile([P, MAX_TILES * P], U32, name=names[0], align_bytes=MX_ALIGN)
+            scales = work.tile([P, MAX_TILES * P], U8, name=names[1], align_bytes=MX_ALIGN)
             nc.vector.quantize_mx(
                 out=codes[:, :rows].bitcast(FP8X4),
                 scales=scales[:, :rows],
@@ -214,7 +215,7 @@ def tile_attentionfreetransformerencoder_pb_t_kernel(tc, h, yt, Wq, bq, Wo, bo, 
 
         def apply_gate(c, first_tile, tiles):
             if first_tile == 0:
-                grouped = work.tile([P, MAX_TILES * P * PACK], BF16, name="y_grouped", align_bytes=64)
+                grouped = work.tile([P, MAX_TILES * P * PACK], BF16, name="y_grouped", align_bytes=MX_ALIGN)
                 y_grouped[c] = grouped
             chunk = CHUNK_TILES[c] * P
             first, rows = first_tile * P, tiles * P

from contextlib import ExitStack

import concourse.mybir as mybir
from concourse.masks import make_identity

F32 = mybir.dt.float32
BF16 = mybir.dt.bfloat16
U32 = mybir.dt.uint32
U8 = mybir.dt.uint8
FP8X4 = mybir.dt.float8_e4m3fn_x4
SIGMOID = mybir.ActivationFunctionType.Sigmoid
ADD = mybir.AluOpType.add
MULT = mybir.AluOpType.mult

ROWS = 8 * 1024
D = 512
P = 128
PACK = 4
CHUNK_TILES = (2,) + (4,) * 15 + (2,)
CHUNKS = len(CHUNK_TILES)
FIRST_TILE = tuple(sum(CHUNK_TILES[:c]) for c in range(CHUNKS))
ROW_TILES = ROWS // P
MAX_TILES = max(CHUNK_TILES)
UNIT_TILES = 2
LINE = 4
BANK = 512
MX_ALIGN = 256
LOOKAHEAD = 6

AT_PROJECT_Q = 1
AT_GATE = 2
AT_PROJECT_OUT = 3

FLOPS = 2 * 2 * ROWS * D * D


def tile_attentionfreetransformerencoder_pb_t_kernel(tc, h, yt, Wq, bq, Wo, bo, out):
    nc = tc.nc

    def chunk_rows(dram, c):
        first = FIRST_TILE[c] * P
        rows = dram.flatten_outer_dims()[first : first + CHUNK_TILES[c] * P, :]
        return rows.rearrange("(p j) d -> p (j d)", p=P)

    with ExitStack() as ctx:
        ctx.enter_context(tc.manual_schedule())

        consts = ctx.enter_context(tc.tile_pool(name="consts", bufs=1))
        rows_in = ctx.enter_context(tc.tile_pool(name="rows_in", bufs=LOOKAHEAD + 1))
        work = ctx.enter_context(tc.tile_pool(name="work", bufs=3))
        rows_out = ctx.enter_context(tc.tile_pool(name="rows_out", bufs=4))
        for_scalar = ctx.enter_context(tc.psum_pool(name="for_scalar", bufs=5))
        for_vector = ctx.enter_context(tc.psum_pool(name="for_vector", bufs=3))

        def scalar_bank():
            bank = for_scalar.tile([P, BANK], F32, name="scalar_bank")
            return bank

        def vector_bank():
            bank = for_vector.tile([P, BANK], F32, name="vector_bank")
            return bank

        h_rows = {}
        yt_rows = {}

        def load_h(c):
            h_sb = rows_in.tile([P, MAX_TILES * D], BF16, name="h_sb")
            nc.sync.dma_start(out=h_sb[:, : CHUNK_TILES[c] * D], in_=chunk_rows(h, c))
            h_rows[c] = h_sb

        def load_yt(c):
            yt_sb = rows_in.tile([P, MAX_TILES * D], BF16, name="yt_sb")
            nc.sync.dma_start(out=yt_sb[:, : CHUNK_TILES[c] * D], in_=chunk_rows(yt, c))
            yt_rows[c] = yt_sb

        def load_weight(w, name):
            raw = consts.tile([P, PACK * D], BF16, name=name)
            nc.sync.dma_start(out=raw[:], in_=w.rearrange("(p t) c -> p (t c)", t=PACK))
            return raw

        warm = consts.tile([P, 1], F32, name="warm")
        nc.vector.memset(warm[:], 0.0)
        nc.scalar.activation(out=warm[:], in_=warm[:], func=SIGMOID)

        ident = consts.tile([P, P], F32, name="ident")
        make_identity(nc, ident[:])
        bo_rows = consts.tile([P, D], BF16, name="bo_rows")
        nc.gpsimd.memset(bo_rows[:], 0.0)
        ones = consts.tile([P, P], BF16, name="ones")
        nc.gpsimd.memset(ones[:], 1.0)

        wq_raw = load_weight(Wq, "wq_raw")
        load_h(0)
        bq_cols = consts.tile([P, PACK], BF16, name="bq_cols")
        nc.sync.dma_start(out=bq_cols[:], in_=bq.rearrange("(p m) -> p m", m=PACK))
        for c in range(1, AT_GATE):
            load_h(c)
        for s in range(AT_GATE, LOOKAHEAD):
            load_yt(s - AT_GATE)
            load_h(s)
            if s == AT_GATE:
                wo_raw = load_weight(Wo, "wo_raw")
                nc.sync.dma_start(out=bo_rows[0:1, :], in_=bo.rearrange("(o d) -> o d", o=1))

        wq_grouped = consts.tile([P, D * PACK], BF16, name="wq_grouped", align_bytes=MX_ALIGN)
        wq_from = wq_raw[:].rearrange("p (t q m) -> p m q t", t=PACK, m=PACK)
        wq_to = wq_grouped[:].rearrange("p (m q t) -> p m q t", m=PACK, t=PACK)
        for m in range(PACK):
            nc.vector.tensor_copy(out=wq_to[:, m], in_=wq_from[:, m])
        wq_codes = consts.tile([P, D], U32, name="wq_codes", align_bytes=MX_ALIGN)
        wq_scales = consts.tile([P, D], U8, name="wq_scales", align_bytes=MX_ALIGN)
        nc.vector.quantize_mx(out=wq_codes[:].bitcast(FP8X4), scales=wq_scales[:], in_=wq_grouped[:])

        wo_grouped = consts.tile([P, D * PACK], BF16, name="wo_grouped", align_bytes=MX_ALIGN)
        wo_codes = consts.tile([P, D], U32, name="wo_codes", align_bytes=MX_ALIGN)
        wo_scales = consts.tile([P, D], U8, name="wo_scales", align_bytes=MX_ALIGN)
        bo_all = consts.tile([P, D], F32, name="bo_all")

        def group_wo():
            nc.vector.tensor_copy(
                out=wo_grouped[:].rearrange("p (c t) -> p c t", t=PACK),
                in_=wo_raw[:].rearrange("p (t c) -> p c t", t=PACK),
            )

        def quantise_wo():
            nc.vector.quantize_mx(
                out=wo_codes[:].bitcast(FP8X4), scales=wo_scales[:], in_=wo_grouped[:]
            )
            bo_ps = vector_bank()
            nc.tensor.matmul(out=bo_ps[:], lhsT=ones[:], rhs=bo_rows[:], start=True, stop=True)
            nc.vector.tensor_copy(out=bo_all[:], in_=bo_ps[:])

        def units(c):
            tiles = CHUNK_TILES[c]
            return [(j, min(UNIT_TILES, tiles - j)) for j in range(0, tiles, UNIT_TILES)]

        def transpose_words(planes, rows_sb, first_tile):
            words = rows_sb[:].bitcast(F32)
            for j in range(len(planes[0])):
                first = (first_tile + j) * (D // 2)
                for u in range(2):
                    nc.tensor.transpose(
                        planes[u][j], words[:, first + u : first + D // 2 : 2], ident[:]
                    )

        h_grouped = {}
        h_mx = {}
        yt_banks = {}
        gates = {}
        y_grouped = {}
        y_mx = {}
        out_rows = {}

        def transpose_h(c, first_tile, tiles):
            if first_tile == 0:
                grouped = work.tile([P, MAX_TILES * P * PACK], BF16, name="h_grouped", align_bytes=MX_ALIGN)
                h_grouped[c] = grouped
            words = tiles * 2 * P
            bank = scalar_bank()
            plane = bank[:, :words].rearrange("p (u j r) -> p u j r", u=2, j=tiles)
            transpose_words([[plane[:, u, j] for j in range(tiles)] for u in range(2)], h_rows[c], first_tile)
            start = first_tile * 2 * P
            nc.scalar.copy(
                out=h_grouped[c][:]
                .bitcast(F32)[:, start : start + words]
                .rearrange("p (r u) -> p r u", u=2),
                in_=bank[:, :words].rearrange("p (u r) -> p r u", u=2),
            )

        def quantise(grouped, c, names):
            rows = CHUNK_TILES[c] * P
            codes = work.tile([P, MAX_TILES * P], U32, name=names[0], align_bytes=MX_ALIGN)
            scales = work.tile([P, MAX_TILES * P], U8, name=names[1], align_bytes=MX_ALIGN)
            nc.vector.quantize_mx(
                out=codes[:, :rows].bitcast(FP8X4),
                scales=scales[:, :rows],
                in_=grouped[:, : rows * PACK],
            )
            return codes, scales

        def quantise_h(c):
            h_mx[c] = quantise(h_grouped[c], c, ("h_codes", "h_scales"))

        def project_q(c, m):
            rows = CHUNK_TILES[c] * P
            if m == 0:
                gate = work.tile([P, PACK * MAX_TILES * P], F32, name="gate")
                gates[c] = gate
            codes, scales = h_mx[c]
            q_ps = scalar_bank()
            nc.tensor.matmul_mx(
                out=q_ps[:, :rows],
                lhsT=wq_codes[:, m * P : (m + 1) * P].bitcast(FP8X4),
                lhsT_scale=wq_scales[:, m * P : (m + 1) * P],
                rhs=codes[:, :rows].bitcast(FP8X4),
                rhs_scale=scales[:, :rows],
                start=True,
                stop=True,
            )
            nc.scalar.activation(
                out=gates[c][:, m * rows : (m + 1) * rows],
                in_=q_ps[:, :rows],
                func=SIGMOID,
                bias=bq_cols[:, m : m + 1],
                scale=1.0,
            )

        def transpose_yt(c, first_tile, tiles):
            bank = vector_bank()
            plane = bank[:, : tiles * 2 * P].rearrange(
                "p (j c u i) -> p u j c i", j=tiles, u=2, i=LINE
            )
            transpose_words([[plane[:, u, j] for j in range(tiles)] for u in range(2)], yt_rows[c], first_tile)
            yt_banks[(c, first_tile)] = bank

        def apply_gate(c, first_tile, tiles):
            if first_tile == 0:
                grouped = work.tile([P, MAX_TILES * P * PACK], BF16, name="y_grouped", align_bytes=MX_ALIGN)
                y_grouped[c] = grouped
            chunk = CHUNK_TILES[c] * P
            first, rows = first_tile * P, tiles * P
            nc.vector.tensor_tensor(
                out=y_grouped[c][:, first * PACK : (first + rows) * PACK].rearrange(
                    "p (c i u e) -> p c u e i", i=LINE, u=2, e=2
                ),
                in0=gates[c][:, : PACK * chunk].rearrange(
                    "p (u e c i) -> p c u e i", u=2, e=2, i=LINE
                )[:, first // LINE : (first + rows) // LINE],
                in1=yt_banks[(c, first_tile)][:, : 2 * rows]
                .bitcast(BF16)
                .rearrange("p (c u i e) -> p c u e i", u=2, i=LINE, e=2),
                op=MULT,
            )

        def quantise_y(c):
            y_mx[c] = quantise(y_grouped[c], c, ("y_codes", "y_scales"))

        def project_out(c, j):
            if j == 0:
                o_sb = rows_out.tile([P, MAX_TILES * D], F32, name="o_sb")
                out_rows[c] = o_sb
            codes, scales = y_mx[c]
            tile_index = FIRST_TILE[c] + j
            through_vector = (tile_index % 2 == 0) != (tile_index >= ROW_TILES - 2)
            o_ps = vector_bank() if through_vector else scalar_bank()
            nc.tensor.matmul_mx(
                out=o_ps[:],
                lhsT=codes[:, j * P : (j + 1) * P].bitcast(FP8X4),
                lhsT_scale=scales[:, j * P : (j + 1) * P],
                rhs=wo_codes[:].bitcast(FP8X4),
                rhs_scale=wo_scales[:],
                start=True,
                stop=True,
            )
            dest = out_rows[c][:, j * D : (j + 1) * D]
            if through_vector:
                nc.vector.tensor_tensor(out=dest, in0=o_ps[:], in1=bo_all[:], op=ADD)
            else:
                nc.scalar.copy(out=dest, in_=o_ps[:])
                nc.gpsimd.tensor_tensor(out=dest, in0=dest, in1=bo_all[:], op=ADD)
            if j % 2 == 1 or CHUNK_TILES[c] == 1:
                done = slice((j // 2) * 2 * D, (j + 1) * D)
                nc.sync.dma_start(out=chunk_rows(out, c)[:, done], in_=out_rows[c][:, done])

        def live(c):
            return 0 <= c < CHUNKS

        for s in range(CHUNKS + AT_PROJECT_OUT):
            if live(s + LOOKAHEAD):
                load_h(s + LOOKAHEAD)
            if live(s - AT_GATE + LOOKAHEAD):
                load_yt(s - AT_GATE + LOOKAHEAD)
            for half in range(2):
                if live(s - AT_GATE) and half < len(units(s - AT_GATE)):
                    transpose_yt(s - AT_GATE, *units(s - AT_GATE)[half])
                    apply_gate(s - AT_GATE, *units(s - AT_GATE)[half])
                if live(s) and half < len(units(s)):
                    transpose_h(s, *units(s)[half])
            if live(s):
                quantise_h(s)
            if live(s - AT_PROJECT_Q):
                for m in range(PACK):
                    project_q(s - AT_PROJECT_Q, m)
            if live(s - AT_PROJECT_OUT):
                project_out(s - AT_PROJECT_OUT, 0)
            if live(s - AT_GATE):
                quantise_y(s - AT_GATE)
            if live(s - AT_PROJECT_OUT):
                for j in range(1, CHUNK_TILES[s - AT_PROJECT_OUT]):
                    project_out(s - AT_PROJECT_OUT, j)
            if s == AT_PROJECT_Q:
                group_wo()
            if s == AT_GATE:
                quantise_wo()
